import numpy as np
import ml_dtypes

BF16 = ml_dtypes.bfloat16


def bf(x):
    return np.asarray(x, np.float32).astype(BF16)


def f32(x):
    return np.asarray(x, np.float32)


def f64(x):
    return np.asarray(x).astype(np.float64)


def striped(idx):
    return np.tile(idx.reshape(-1, 16).T, (8, 1))


D, S, Q, N = 128, 512, 384, 256


def setup_inputs():
    return {'table': bf(np.random.standard_normal((D, S))), 'w': bf(np.random.standard_normal((D, Q)) / np.sqrt(D)), 'b': f32(0.1 * np.random.standard_normal((Q, 1))), 'offs': striped(np.random.permutation(np.tile(np.arange(S), 2))[:N])}


def reference(table, w, b, offs):
    idx = offs[:16].T.reshape(-1)
    x = f64(table)[:, idx]
    return np.concatenate([f64(w).T @ x + f64(b), x], axis=0)

@@ -1,0 +1,55 @@
+import concourse.mybir as mybir
+from concourse.masks import make_identity
+
+BF16, F32, U16 = mybir.dt.bfloat16, mybir.dt.float32, mybir.dt.uint16
+
+P = 128
+S = 512
+Q = 384
+N = 256
+PROJECTIONS = Q // P
+
+FLOPS = 2 * P * Q * N
+
+
+def tile_gteprogramclassification_kernel(tc, table, w, b, offs, out):
+    nc = tc.nc
+    out_blocks = out.rearrange("(t p) n -> t p n", p=P)
+
+    with (
+        tc.tile_pool(name="held", bufs=1) as held,
+        tc.tile_pool(name="staged", bufs=PROJECTIONS + 1) as staged,
+        tc.psum_pool(name="psum", bufs=PROJECTIONS + 1) as psum,
+    ):
+        offsets = held.tile([P, N // 16], U16, name="offsets")
+        nc.sync.dma_start(offsets[:], offs)
+        table_sb = held.tile([P, S], BF16, name="table_sb")
+        nc.scalar.dma_start(table_sb[:], table)
+        w_sb = held.tile([P, Q], BF16, name="w_sb")
+        nc.sync.dma_start(w_sb[:], w)
+        bias = held.tile([P, PROJECTIONS], F32, name="bias")
+        with nc.allow_non_contiguous_dma(reason="384 single float32 values, one bias to a partition"):
+            nc.scalar.dma_start(bias[:], b.rearrange("(t p) o -> p (t o)", p=P))
+
+        identity = held.tile([P, P], BF16, name="identity")
+        make_identity(nc, identity[:])
+
+        gathered_ps = psum.tile([P, N], F32, name="product")
+        nc.tensor.matmul(gathered_ps[:], identity[:], table_sb[:].indirect(offsets[:]), start=True, stop=True)
+        gathered = staged.tile([P, N], F32, name="block")
+        nc.vector.tensor_copy(gathered[:], gathered_ps[:])
+        nc.sync.dma_start(out_blocks[PROJECTIONS], gathered[:])
+
+        for t in range(PROJECTIONS):
+            product = psum.tile([P, N], F32, name="product")
+            nc.tensor.matmul(
+                product[:], w_sb[:, t * P : (t + 1) * P], table_sb[:].indirect(offsets[:]), start=True, stop=True
+            )
+            block = staged.tile([P, N], F32, name="block")
+            if t % 2 == 0:
+                nc.scalar.activation(
+                    block[:], product[:], mybir.ActivationFunctionType.Identity, bias=bias[:, t : t + 1]
+                )
+            else:
+                nc.vector.tensor_scalar_add(block[:], product[:], bias[:, t : t + 1])
+            nc.sync.dma_start(out_blocks[t], block[:])

@@ -34,6 +34,11 @@ def tile_gteprogramclassification_kernel(tc, table, w, b, offs, out):
         identity = held.tile([P, P], BF16, name="identity")
         make_identity(nc, identity[:])
 
+        scratch = held.tile([P, 1], F32, name="scratch")
+        nc.vector.memset(scratch[:], 0.0)
+        table_loaded = held.tile([P, 1], F32, name="table_loaded")
+        nc.scalar.activation(table_loaded[:], scratch[:], mybir.ActivationFunctionType.Identity)
+
         gathered_ps = psum.tile([P, N], F32, name="product")
         nc.tensor.matmul(gathered_ps[:], identity[:], table_sb[:].indirect(offsets[:]), start=True, stop=True)
         gathered = staged.tile([P, N], F32, name="block")

@@ -8,6 +8,8 @@ S = 512
 Q = 384
 N = 256
 PROJECTIONS = Q // P
+WARM_COLUMNS = 512
+WARM_MATMULS = 4
 
 FLOPS = 2 * P * Q * N
 
@@ -38,6 +40,12 @@ def tile_gteprogramclassification_kernel(tc, table, w, b, offs, out):
         nc.vector.memset(scratch[:], 0.0)
         table_loaded = held.tile([P, 1], F32, name="table_loaded")
         nc.scalar.activation(table_loaded[:], scratch[:], mybir.ActivationFunctionType.Identity)
+
+        zeros = held.tile([P, WARM_COLUMNS], BF16, name="zeros")
+        nc.vector.memset(zeros[:], 0.0)
+        unused = psum.tile([P, WARM_COLUMNS], F32, name="unused")
+        for _ in range(WARM_MATMULS):
+            nc.tensor.matmul(unused[:], zeros[:, 0:P], zeros[:], start=True, stop=True)
 
         gathered_ps = psum.tile([P, N], F32, name="product")
         nc.tensor.matmul(gathered_ps[:], identity[:], table_sb[:].indirect(offsets[:]), start=True, stop=True)

@@ -8,8 +8,6 @@ S = 512
 Q = 384
 N = 256
 PROJECTIONS = Q // P
-WARM_COLUMNS = 512
-WARM_MATMULS = 4
 
 FLOPS = 2 * P * Q * N
 
@@ -31,7 +29,7 @@ def tile_gteprogramclassification_kernel(tc, table, w, b, offs, out):
         nc.sync.dma_start(w_sb[:], w)
         bias = held.tile([P, PROJECTIONS], F32, name="bias")
         with nc.allow_non_contiguous_dma(reason="384 single float32 values, one bias to a partition"):
-            nc.scalar.dma_start(bias[:], b.rearrange("(t p) o -> p (t o)", p=P))
+            nc.sync.dma_start(bias[:], b.rearrange("(t p) o -> p (t o)", p=P))
 
         identity = held.tile([P, P], BF16, name="identity")
         make_identity(nc, identity[:])
@@ -40,12 +38,6 @@ def tile_gteprogramclassification_kernel(tc, table, w, b, offs, out):
         nc.vector.memset(scratch[:], 0.0)
         table_loaded = held.tile([P, 1], F32, name="table_loaded")
         nc.scalar.activation(table_loaded[:], scratch[:], mybir.ActivationFunctionType.Identity)
-
-        zeros = held.tile([P, WARM_COLUMNS], BF16, name="zeros")
-        nc.vector.memset(zeros[:], 0.0)
-        unused = psum.tile([P, WARM_COLUMNS], F32, name="unused")
-        for _ in range(WARM_MATMULS):
-            nc.tensor.matmul(unused[:], zeros[:, 0:P], zeros[:], start=True, stop=True)
 
         gathered_ps = psum.tile([P, N], F32, name="product")
         nc.tensor.matmul(gathered_ps[:], identity[:], table_sb[:].indirect(offsets[:]), start=True, stop=True)

@@ -8,6 +8,7 @@ S = 512
 Q = 384
 N = 256
 PROJECTIONS = Q // P
+BLOCK = 32
 
 FLOPS = 2 * P * Q * N
 
@@ -27,9 +28,16 @@ def tile_gteprogramclassification_kernel(tc, table, w, b, offs, out):
         nc.scalar.dma_start(table_sb[:], table)
         w_sb = held.tile([P, Q], BF16, name="w_sb")
         nc.sync.dma_start(w_sb[:], w)
-        bias = held.tile([P, PROJECTIONS], F32, name="bias")
-        with nc.allow_non_contiguous_dma(reason="384 single float32 values, one bias to a partition"):
-            nc.sync.dma_start(bias[:], b.rearrange("(t p) o -> p (t o)", p=P))
+
+        b_runs = held.tile([P, P], F32, name="b_runs", align_bytes=64)
+        nc.gpsimd.memset(b_runs[:], 0.0)
+        first_rows = b_runs[:].rearrange("(g j) c -> j g c", j=BLOCK)[0]
+        nc.sync.dma_start(
+            first_rows[:, 0 : PROJECTIONS * BLOCK].rearrange("g (t i) -> g t i", i=BLOCK),
+            b.rearrange("(t g i) o -> g t (i o)", g=P // BLOCK, i=BLOCK),
+        )
+        bias = held.tile([P, P], F32, name="bias", align_bytes=64)
+        nc.vector.transpose(bias[:], b_runs[:])
 
         identity = held.tile([P, P], BF16, name="identity")
         make_identity(nc, identity[:])
@@ -53,8 +61,8 @@ def tile_gteprogramclassification_kernel(tc, table, w, b, offs, out):
             block = staged.tile([P, N], F32, name="block")
             if t % 2 == 0:
                 nc.scalar.activation(
-                    block[:], product[:], mybir.ActivationFunctionType.Identity, bias=bias[:, t : t + 1]
+                    block[:], product[:], mybir.ActivationFunctionType.Identity, bias=bias[:, t * BLOCK : t * BLOCK + 1]
                 )
             else:
-                nc.vector.tensor_scalar_add(block[:], product[:], bias[:, t : t + 1])
+                nc.vector.tensor_scalar_add(block[:], product[:], bias[:, t * BLOCK : t * BLOCK + 1])
             nc.sync.dma_start(out_blocks[t], block[:])

@@ -2,42 +2,36 @@ import concourse.mybir as mybir
 from concourse.masks import make_identity
 
 BF16, F32, U16 = mybir.dt.bfloat16, mybir.dt.float32, mybir.dt.uint16
+IDENTITY = mybir.ActivationFunctionType.Identity
 
 P = 128
 S = 512
 Q = 384
 N = 256
 PROJECTIONS = Q // P
-BLOCK = 32
 
 FLOPS = 2 * P * Q * N
 
 
 def tile_gteprogramclassification_kernel(tc, table, w, b, offs, out):
     nc = tc.nc
-    out_blocks = out.rearrange("(t p) n -> t p n", p=P)
+    projected_rows = out[0:Q, :].rearrange("(t p) n -> t p n", p=P)
+    residual_rows = out[Q : Q + P, :]
 
     with (
         tc.tile_pool(name="held", bufs=1) as held,
         tc.tile_pool(name="staged", bufs=PROJECTIONS + 1) as staged,
         tc.psum_pool(name="psum", bufs=PROJECTIONS + 1) as psum,
     ):
+        table_sb = held.tile([P, S], BF16, name="table_sb")
+        nc.sync.dma_start(table_sb[:], table)
         offsets = held.tile([P, N // 16], U16, name="offsets")
         nc.sync.dma_start(offsets[:], offs)
-        table_sb = held.tile([P, S], BF16, name="table_sb")
-        nc.scalar.dma_start(table_sb[:], table)
         w_sb = held.tile([P, Q], BF16, name="w_sb")
         nc.sync.dma_start(w_sb[:], w)
-
-        b_runs = held.tile([P, P], F32, name="b_runs", align_bytes=64)
-        nc.gpsimd.memset(b_runs[:], 0.0)
-        first_rows = b_runs[:].rearrange("(g j) c -> j g c", j=BLOCK)[0]
-        nc.sync.dma_start(
-            first_rows[:, 0 : PROJECTIONS * BLOCK].rearrange("g (t i) -> g t i", i=BLOCK),
-            b.rearrange("(t g i) o -> g t (i o)", g=P // BLOCK, i=BLOCK),
-        )
-        bias = held.tile([P, P], F32, name="bias", align_bytes=64)
-        nc.vector.transpose(bias[:], b_runs[:])
+        bias = held.tile([P, PROJECTIONS], F32, name="bias")
+        with nc.allow_non_contiguous_dma(reason="384 single float32 values, one bias to a partition"):
+            nc.scalar.dma_start(bias[:], b.rearrange("(t p) o -> p (t o)", p=P))
 
         identity = held.tile([P, P], BF16, name="identity")
         make_identity(nc, identity[:])
@@ -45,24 +39,22 @@ def tile_gteprogramclassification_kernel(tc, table, w, b, offs, out):
         scratch = held.tile([P, 1], F32, name="scratch")
         nc.vector.memset(scratch[:], 0.0)
         table_loaded = held.tile([P, 1], F32, name="table_loaded")
-        nc.scalar.activation(table_loaded[:], scratch[:], mybir.ActivationFunctionType.Identity)
+        nc.scalar.activation(table_loaded[:], scratch[:], IDENTITY)
 
-        gathered_ps = psum.tile([P, N], F32, name="product")
-        nc.tensor.matmul(gathered_ps[:], identity[:], table_sb[:].indirect(offsets[:]), start=True, stop=True)
-        gathered = staged.tile([P, N], F32, name="block")
-        nc.vector.tensor_copy(gathered[:], gathered_ps[:])
-        nc.sync.dma_start(out_blocks[PROJECTIONS], gathered[:])
+        product = psum.tile([P, N], F32, name="product")
+        nc.tensor.matmul(product[:], identity[:], table_sb[:].indirect(offsets[:]), start=True, stop=True)
+        rows = staged.tile([P, N], F32, name="rows")
+        nc.vector.tensor_copy(rows[:], product[:])
+        nc.sync.dma_start(residual_rows, rows[:])
 
         for t in range(PROJECTIONS):
             product = psum.tile([P, N], F32, name="product")
             nc.tensor.matmul(
                 product[:], w_sb[:, t * P : (t + 1) * P], table_sb[:].indirect(offsets[:]), start=True, stop=True
             )
-            block = staged.tile([P, N], F32, name="block")
+            rows = staged.tile([P, N], F32, name="rows")
             if t % 2 == 0:
-                nc.scalar.activation(
-                    block[:], product[:], mybir.ActivationFunctionType.Identity, bias=bias[:, t * BLOCK : t * BLOCK + 1]
-                )
+                nc.scalar.activation(rows[:], product[:], IDENTITY, bias=bias[:, t : t + 1])
             else:
-                nc.vector.tensor_scalar_add(block[:], product[:], bias[:, t * BLOCK : t * BLOCK + 1])
-            nc.sync.dma_start(out_blocks[t], block[:])
+                nc.vector.tensor_scalar_add(rows[:], product[:], bias[:, t : t + 1])
+            nc.sync.dma_start(projected_rows[t], rows[:])

@@ -23,10 +23,10 @@ def tile_gteprogramclassification_kernel(tc, table, w, b, offs, out):
         tc.tile_pool(name="staged", bufs=PROJECTIONS + 1) as staged,
         tc.psum_pool(name="psum", bufs=PROJECTIONS + 1) as psum,
     ):
-        table_sb = held.tile([P, S], BF16, name="table_sb")
-        nc.sync.dma_start(table_sb[:], table)
         offsets = held.tile([P, N // 16], U16, name="offsets")
         nc.sync.dma_start(offsets[:], offs)
+        table_sb = held.tile([P, S], BF16, name="table_sb")
+        nc.scalar.dma_start(table_sb[:], table)
         w_sb = held.tile([P, Q], BF16, name="w_sb")
         nc.sync.dma_start(w_sb[:], w)
         bias = held.tile([P, PROJECTIONS], F32, name="bias")
@@ -55,6 +55,7 @@ def tile_gteprogramclassification_kernel(tc, table, w, b, offs, out):
             rows = staged.tile([P, N], F32, name="rows")
             if t % 2 == 0:
                 nc.scalar.activation(rows[:], product[:], IDENTITY, bias=bias[:, t : t + 1])
+                nc.scalar.dma_start(projected_rows[t], rows[:])
             else:
                 nc.vector.tensor_scalar_add(rows[:], product[:], bias[:, t : t + 1])
-            nc.sync.dma_start(projected_rows[t], rows[:])
+                nc.sync.dma_start(projected_rows[t], rows[:])

@@ -53,9 +53,8 @@ def tile_gteprogramclassification_kernel(tc, table, w, b, offs, out):
                 product[:], w_sb[:, t * P : (t + 1) * P], table_sb[:].indirect(offsets[:]), start=True, stop=True
             )
             rows = staged.tile([P, N], F32, name="rows")
-            if t % 2 == 0:
-                nc.scalar.activation(rows[:], product[:], IDENTITY, bias=bias[:, t : t + 1])
-                nc.scalar.dma_start(projected_rows[t], rows[:])
-            else:
+            if t == 0:
                 nc.vector.tensor_scalar_add(rows[:], product[:], bias[:, t : t + 1])
-                nc.sync.dma_start(projected_rows[t], rows[:])
+            else:
+                nc.scalar.activation(rows[:], product[:], IDENTITY, bias=bias[:, t : t + 1])
+            nc.sync.dma_start(projected_rows[t], rows[:])

import concourse.mybir as mybir
from concourse.masks import make_identity

BF16, F32, U16 = mybir.dt.bfloat16, mybir.dt.float32, mybir.dt.uint16
IDENTITY = mybir.ActivationFunctionType.Identity

P = 128
S = 512
Q = 384
N = 256
PROJECTIONS = Q // P

FLOPS = 2 * P * Q * N


def tile_gteprogramclassification_kernel(tc, table, w, b, offs, out):
    nc = tc.nc
    projected_rows = out[0:Q, :].rearrange("(t p) n -> t p n", p=P)
    residual_rows = out[Q : Q + P, :]

    with (
        tc.tile_pool(name="held", bufs=1) as held,
        tc.tile_pool(name="staged", bufs=PROJECTIONS + 1) as staged,
        tc.psum_pool(name="psum", bufs=PROJECTIONS + 1) as psum,
    ):
        offsets = held.tile([P, N // 16], U16, name="offsets")
        nc.sync.dma_start(offsets[:], offs)
        table_sb = held.tile([P, S], BF16, name="table_sb")
        nc.scalar.dma_start(table_sb[:], table)
        w_sb = held.tile([P, Q], BF16, name="w_sb")
        nc.sync.dma_start(w_sb[:], w)
        bias = held.tile([P, PROJECTIONS], F32, name="bias")
        with nc.allow_non_contiguous_dma(reason="384 single float32 values, one bias to a partition"):
            nc.scalar.dma_start(bias[:], b.rearrange("(t p) o -> p (t o)", p=P))

        identity = held.tile([P, P], BF16, name="identity")
        make_identity(nc, identity[:])

        scratch = held.tile([P, 1], F32, name="scratch")
        nc.vector.memset(scratch[:], 0.0)
        table_loaded = held.tile([P, 1], F32, name="table_loaded")
        nc.scalar.activation(table_loaded[:], scratch[:], IDENTITY)

        product = psum.tile([P, N], F32, name="product")
        nc.tensor.matmul(product[:], identity[:], table_sb[:].indirect(offsets[:]), start=True, stop=True)
        rows = staged.tile([P, N], F32, name="rows")
        nc.vector.tensor_copy(rows[:], product[:])
        nc.sync.dma_start(residual_rows, rows[:])

        for t in range(PROJECTIONS):
            product = psum.tile([P, N], F32, name="product")
            nc.tensor.matmul(
                product[:], w_sb[:, t * P : (t + 1) * P], table_sb[:].indirect(offsets[:]), start=True, stop=True
            )
            rows = staged.tile([P, N], F32, name="rows")
            if t == 0:
                nc.vector.tensor_scalar_add(rows[:], product[:], bias[:, t : t + 1])
            else:
                nc.scalar.activation(rows[:], product[:], IDENTITY, bias=bias[:, t : t + 1])
            nc.sync.dma_start(projected_rows[t], rows[:])
